import numpy as np
import ml_dtypes


def mxq(x, axis, fmt="e4m3"):
    dtype, down = {"e4m3": (ml_dtypes.float8_e4m3fn, 7), "e5m2": (ml_dtypes.float8_e5m2, 14)}[fmt]
    v = np.moveaxis(np.asarray(x, np.float32).astype(ml_dtypes.bfloat16).astype(np.float64), axis, -1)
    blocks = v.reshape(v.shape[:-1] + (-1, 32))
    amax = np.abs(blocks).max(-1, keepdims=True)
    byte = np.maximum(np.where(amax > 0, np.frexp(amax)[1] - 1 + 127, 0) - down, 1)
    scale = np.exp2(byte - 127.0)
    codes = (blocks / scale).astype(np.float32).astype(dtype).astype(np.float64)
    return np.moveaxis((codes * scale).reshape(v.shape), -1, axis)


WIDE = False


def mx_kscale(k):
    if not WIDE:
        return np.ones(k)
    levels = np.array([10, -10, 5, -5, 0])
    a = np.random.permutation(np.resize(levels, k // 512 * 4)).reshape(k // 512, 4)
    idx = np.arange(k)
    return np.exp2(a[idx // 512, idx % 128 // 32])


BF16 = ml_dtypes.bfloat16


def bf(x):
    return np.asarray(x, np.float32).astype(BF16)


def f64(x):
    return np.asarray(x).astype(np.float64)


S, A, B, K, H, G = 4, 8, 16, 1024, 1024, 3


def sigmoid(v):
    return 1.0 / (1.0 + np.exp(-v))


def setup_inputs():
    s = mx_kscale(K)
    c = 0.7 / np.sqrt(K)
    return {"x": bf(np.random.standard_normal((S + 1, A, B, K)) * s),
            "x_mix": bf(np.random.standard_normal((S + 1, A, B, H))),
            "WL": bf(np.random.standard_normal((H, K)) * c / s),
            "WR": bf(np.random.standard_normal((H, K)) * c / s),
            "GL": bf(np.random.standard_normal((G * H, K)) * c / s),
            "GR": bf(np.random.standard_normal((G * H, K)) * c / s)}


def reference(x, x_mix, WL, WR, GL, GR):
    xm = f64(x_mix)
    left, right = xm[:-1], xm[1:]
    xq = mxq(f64(x), 3, "e4m3")
    lq, rq = xq[:-1], xq[1:]
    center = sigmoid((lq @ mxq(f64(WL), 1, "e4m3").T) + (rq @ mxq(f64(WR), 1, "e4m3").T))
    gate = (lq @ mxq(f64(GL), 1, "e4m3").T) + (rq @ mxq(f64(GR), 1, "e4m3").T)
    g = gate.reshape(gate.shape[:-1] + (G, H))
    e = np.exp(g - g.max(-2, keepdims=True))
    w = e / e.sum(-2, keepdims=True)
    return left * w[..., 0, :] + right * w[..., 1, :] + center * w[..., 2, :]

@@ -1,0 +1,256 @@
+from contextlib import ExitStack
+
+import concourse.mybir as mybir
+from concourse.masks import make_identity
+
+F32 = mybir.dt.float32
+BF16 = mybir.dt.bfloat16
+U32 = mybir.dt.uint32
+U8 = mybir.dt.uint8
+FP8X4 = mybir.dt.float8_e4m3fn_x4
+ACT = mybir.ActivationFunctionType
+ALU = mybir.AluOpType
+
+P = 128
+K = 1024
+H = 1024
+PASSES = 2
+HALVES = 2
+OUT_TILES = 4
+X_TILES = 5
+SIDES = 2
+COLS = 256
+ROW_TILES = COLS // P
+CHUNKS = H // COLS
+PAIRS = OUT_TILES // 2
+
+GATE0, GATE1, GATE2, CENTER = 0, 1, 2, 3
+
+RAW_BUFS = 6
+AHEAD = 2
+
+FLOPS = 2 * OUT_TILES * P * 4 * H * SIDES * K
+
+
+def tile_grconv_pa_kernel(tc, x, x_mix, WL, WR, GL, GR, out):
+    nc = tc.nc
+
+    rounds = []
+    for chunk in range(CHUNKS):
+        rounds.append((GATE0, chunk))
+        rounds.append((GATE1, chunk))
+    for chunk in range(CHUNKS):
+        rounds.append((GATE2, chunk))
+        rounds.append((CENTER, chunk))
+    n_rounds = len(rounds)
+    last_gate1 = 2 * CHUNKS - 1
+
+    x_rows = x.rearrange("s a b k -> (a b) s k")
+    mix_rows = x_mix.rearrange("s a b h -> (a b) s h")
+    out_rows = out.rearrange("s a b h -> (a b) s h")
+
+    with ExitStack() as ctx:
+        ctx.enter_context(tc.manual_schedule())
+        keep = ctx.enter_context(tc.tile_pool(name="keep", bufs=1))
+        raw_pool = ctx.enter_context(tc.tile_pool(name="raw", bufs=RAW_BUFS))
+        stage = ctx.enter_context(tc.tile_pool(name="stage", bufs=3))
+        flip_banks = ctx.enter_context(tc.psum_pool(name="flip", bufs=4))
+        sum_banks = ctx.enter_context(tc.psum_pool(name="sums", bufs=4))
+
+        identity = keep.tile([P, P], F32)
+        make_identity(nc, identity[:])
+        minus_half = keep.tile([P, 1], F32)
+        nc.vector.memset(minus_half[:], -0.5)
+        plus_half = keep.tile([P, 1], F32)
+        nc.vector.memset(plus_half[:], 0.5)
+        warm = keep.tile([P, 1], F32)
+        nc.scalar.activation(out=warm[:], in_=plus_half[:], func=ACT.Sigmoid)
+
+        x_raw = keep.tile([P, X_TILES, K], BF16)
+        x_grouped = keep.tile([P, X_TILES, K], BF16, align_bytes=64)
+        x_codes = keep.tile([P, X_TILES, K // 4], U32, align_bytes=64)
+        x_scales = keep.tile([P, X_TILES, K // 4], U8, align_bytes=64)
+        mix_in = keep.tile([P, X_TILES, H], BF16)
+        ref = keep.tile([P, OUT_TILES, H], F32)
+        gap = keep.tile([P, OUT_TILES, H], F32)
+        share = keep.tile([P, OUT_TILES, H], F32)
+        blend = keep.tile([P, OUT_TILES, H], F32)
+
+        raw_tiles = {}
+        grouped_tiles = {}
+        code_tiles = {}
+        sum_tiles = {}
+        center_tiles = {}
+
+        def load_round(r):
+            kind, chunk = rounds[r]
+            raw = raw_pool.tile([P, SIDES, ROW_TILES, K], BF16, name="raw")
+            raw_tiles[r] = raw
+            pair = (WL, WR) if kind == CENTER else (GL, GR)
+            first = chunk * COLS if kind == CENTER else kind * H + chunk * COLS
+            for side in range(SIDES):
+                nc.sync.dma_start(
+                    out=raw[:, side, :, :],
+                    in_=pair[side][first : first + COLS, :].rearrange("(t p) k -> p t k", p=P),
+                )
+
+        def flip(rows):
+            words = rows.bitcast(F32)
+            bank = flip_banks.tile([P, PASSES, HALVES, P], F32, name="bank")
+            for g in range(PASSES):
+                for u in range(HALVES):
+                    first = (g * HALVES + u) * P
+                    nc.tensor.transpose(bank[:, g, u, :], words[:, first : first + P], identity[:])
+            return bank[:].rearrange("p g u r -> p g r u")
+
+        def transpose_round(r):
+            grouped = stage.tile([P, SIDES * PASSES * COLS * 4], BF16, align_bytes=64, name="grouped")
+            grouped_tiles[r] = grouped
+            words = grouped[:].bitcast(F32).rearrange(
+                "p (s g f u) -> p s g f u", s=SIDES, g=PASSES, u=HALVES
+            )
+            for side in range(SIDES):
+                for t in range(ROW_TILES):
+                    flipped = flip(raw_tiles[r][:, side, t, :])
+                    nc.scalar.copy(out=words[:, side, :, t * P : (t + 1) * P, :], in_=flipped)
+
+        def quantise_round(r):
+            codes = stage.tile([P, SIDES * PASSES * COLS], U32, align_bytes=64, name="codes")
+            scales = stage.tile([P, SIDES * PASSES * COLS], U8, align_bytes=64, name="scales")
+            code_tiles[r] = (codes, scales)
+            nc.vector.quantize_mx(
+                out=codes[:].bitcast(FP8X4), scales=scales[:], in_=grouped_tiles[r][:]
+            )
+
+        def multiply_round(r):
+            codes, scales = code_tiles[r]
+            sums = [sum_banks.tile([P, 2, COLS], F32, name="sums") for pair in range(PAIRS)]
+            sum_tiles[r] = sums
+            for i in range(OUT_TILES):
+                for side in range(SIDES):
+                    for g in range(PASSES):
+                        tokens = slice(g * P, (g + 1) * P)
+                        feats = slice((side * PASSES + g) * COLS, (side * PASSES + g + 1) * COLS)
+                        nc.tensor.matmul_mx(
+                            out=sums[i // 2][:, i % 2, :],
+                            lhsT=x_codes[:, i + side, tokens].bitcast(FP8X4),
+                            lhsT_scale=x_scales[:, i + side, tokens],
+                            rhs=codes[:, feats].bitcast(FP8X4),
+                            rhs_scale=scales[:, feats],
+                            start=(side == 0 and g == 0),
+                            stop=(side == SIDES - 1 and g == PASSES - 1),
+                        )
+
+        def epilogue(r, lag):
+            kind, chunk = rounds[r]
+            cols = slice(chunk * COLS, (chunk + 1) * COLS)
+            halves = [slice(2 * pair, 2 * pair + 2) for pair in range(PAIRS)]
+            if kind == GATE0 and lag == 0:
+                for pair in range(PAIRS):
+                    nc.scalar.copy(out=ref[:, halves[pair], cols], in_=sum_tiles[r][pair][:])
+            if kind == GATE1 and lag == 0:
+                for pair in range(PAIRS):
+                    nc.vector.tensor_tensor(
+                        out=gap[:, halves[pair], cols],
+                        in0=sum_tiles[r][pair][:],
+                        in1=ref[:, halves[pair], cols],
+                        op=ALU.subtract,
+                    )
+            if kind == GATE1 and lag == 1:
+                nc.vector.scalar_tensor_tensor(
+                    out=ref[:, :, cols],
+                    in0=gap[:, :, cols],
+                    scalar=0.0,
+                    in1=ref[:, :, cols],
+                    op0=ALU.max,
+                    op1=ALU.add,
+                )
+                nc.scalar.activation(out=share[:, :, cols], in_=gap[:, :, cols], func=ACT.Sigmoid)
+            if kind == GATE1 and lag == 2:
+                nc.scalar.activation(
+                    out=gap[:, :, cols], in_=share[:, :, cols], func=ACT.Abs, bias=minus_half[:]
+                )
+                nc.vector.tensor_tensor(
+                    out=blend[:, :, cols], in0=share[:, :, cols], in1=blend[:, :, cols], op=ALU.mult
+                )
+                if r == last_gate1:
+                    nc.scalar.activation(out=gap[:], in_=gap[:], func=ACT.Ln, bias=plus_half[:])
+            if kind == GATE1 and lag == 3:
+                nc.vector.tensor_tensor(
+                    out=blend[:, :, cols],
+                    in0=blend[:, :, cols],
+                    in1=mix_in[:, 0:OUT_TILES, cols],
+                    op=ALU.add,
+                )
+            if kind == GATE2 and lag == 0:
+                for pair in range(PAIRS):
+                    nc.vector.tensor_tensor(
+                        out=ref[:, halves[pair], cols],
+                        in0=sum_tiles[r][pair][:],
+                        in1=ref[:, halves[pair], cols],
+                        op=ALU.subtract,
+                    )
+            if kind == GATE2 and lag == 2:
+                nc.vector.tensor_tensor(
+                    out=ref[:, :, cols], in0=ref[:, :, cols], in1=gap[:, :, cols], op=ALU.add
+                )
+            if kind == GATE2 and lag == 3:
+                nc.scalar.activation(out=ref[:, :, cols], in_=ref[:, :, cols], func=ACT.Sigmoid)
+            if kind == CENTER and lag == 0:
+                center = stage.tile([P, OUT_TILES, COLS], F32, name="center")
+                center_tiles[r] = center
+                for pair in range(PAIRS):
+                    nc.scalar.activation(
+                        out=center[:, halves[pair], :], in_=sum_tiles[r][pair][:], func=ACT.Sigmoid
+                    )
+            if kind == CENTER and lag == 1:
+                center = center_tiles[r]
+                nc.vector.tensor_tensor(
+                    out=center[:], in0=center[:], in1=blend[:, :, cols], op=ALU.subtract
+                )
+            if kind == CENTER and lag == 3:
+                center = center_tiles[r]
+                for op, other in ((ALU.mult, ref), (ALU.add, blend)):
+                    for pair in range(PAIRS):
+                        nc.vector.tensor_tensor(
+                            out=center[:, halves[pair], :],
+                            in0=center[:, halves[pair], :],
+                            in1=other[:, halves[pair], cols],
+                            op=op,
+                        )
+                nc.sync.dma_start(out=out_rows[:, :, cols], in_=center[:])
+
+        for i in range(X_TILES):
+            nc.sync.dma_start(out=x_raw[:, i, :], in_=x_rows[:, i, :])
+        for r in range(RAW_BUFS):
+            load_round(r)
+            if r == 1:
+                nc.sync.dma_start(out=mix_in[:], in_=mix_rows)
+
+        x_words = x_grouped[:].bitcast(F32).rearrange("p i (g r u) -> p i g r u", g=PASSES, u=HALVES)
+        for i in range(X_TILES):
+            nc.vector.tensor_copy(out=x_words[:, i, :, :, :], in_=flip(x_raw[:, i, :]))
+        for i in range(X_TILES):
+            nc.vector.quantize_mx(
+                out=x_codes[:, i, :].bitcast(FP8X4), scales=x_scales[:, i, :], in_=x_grouped[:, i, :]
+            )
+
+        max_lag = 3
+        for it in range(n_rounds + AHEAD + max_lag + 1):
+            if it < n_rounds:
+                transpose_round(it)
+                if it + RAW_BUFS < n_rounds:
+                    load_round(it + RAW_BUFS)
+            if 0 <= it - 1 < n_rounds:
+                quantise_round(it - 1)
+            if 0 <= it - 1 < OUT_TILES:
+                i = it - 1
+                nc.vector.tensor_tensor(
+                    out=blend[:, i, :], in0=mix_in[:, i + 1, :], in1=mix_in[:, i, :], op=ALU.subtract
+                )
+            for lag in range(1, max_lag + 1):
+                if 0 <= it - AHEAD - lag < n_rounds:
+                    epilogue(it - AHEAD - lag, lag)
+            if 0 <= it - AHEAD < n_rounds:
+                multiply_round(it - AHEAD)
+                epilogue(it - AHEAD, 0)

@@ -27,7 +27,7 @@ PAIRS = OUT_TILES // 2
 GATE0, GATE1, GATE2, CENTER = 0, 1, 2, 3
 
 RAW_BUFS = 6
-AHEAD = 2
+LAST_LAG = 3
 
 FLOPS = 2 * OUT_TILES * P * 4 * H * SIDES * K
 
@@ -44,6 +44,7 @@ def tile_grconv_pa_kernel(tc, x, x_mix, WL, WR, GL, GR, out):
         rounds.append((CENTER, chunk))
     n_rounds = len(rounds)
     last_gate1 = 2 * CHUNKS - 1
+    log_iteration = last_gate1 + 2 + 2
 
     x_rows = x.rearrange("s a b k -> (a b) s k")
     mix_rows = x_mix.rearrange("s a b h -> (a b) s h")
@@ -86,12 +87,12 @@ def tile_grconv_pa_kernel(tc, x, x_mix, WL, WR, GL, GR, out):
             kind, chunk = rounds[r]
             raw = raw_pool.tile([P, SIDES, ROW_TILES, K], BF16, name="raw")
             raw_tiles[r] = raw
-            pair = (WL, WR) if kind == CENTER else (GL, GR)
+            matrices = (WL, WR) if kind == CENTER else (GL, GR)
             first = chunk * COLS if kind == CENTER else kind * H + chunk * COLS
             for side in range(SIDES):
                 nc.sync.dma_start(
                     out=raw[:, side, :, :],
-                    in_=pair[side][first : first + COLS, :].rearrange("(t p) k -> p t k", p=P),
+                    in_=matrices[side][first : first + COLS, :].rearrange("(t p) k -> p t k", p=P),
                 )
 
         def flip(rows):
@@ -112,7 +113,11 @@ def tile_grconv_pa_kernel(tc, x, x_mix, WL, WR, GL, GR, out):
             for side in range(SIDES):
                 for t in range(ROW_TILES):
                     flipped = flip(raw_tiles[r][:, side, t, :])
-                    nc.scalar.copy(out=words[:, side, :, t * P : (t + 1) * P, :], in_=flipped)
+                    target = words[:, side, :, t * P : (t + 1) * P, :]
+                    if r == log_iteration:
+                        nc.vector.tensor_copy(out=target, in_=flipped)
+                    else:
+                        nc.scalar.copy(out=target, in_=flipped)
 
         def quantise_round(r):
             codes = stage.tile([P, SIDES * PASSES * COLS], U32, align_bytes=64, name="codes")
@@ -121,6 +126,18 @@ def tile_grconv_pa_kernel(tc, x, x_mix, WL, WR, GL, GR, out):
             nc.vector.quantize_mx(
                 out=codes[:].bitcast(FP8X4), scales=scales[:], in_=grouped_tiles[r][:]
             )
+
+        def prepare_x():
+            words = x_grouped[:].bitcast(F32).rearrange(
+                "p i (g r u) -> p i g r u", g=PASSES, u=HALVES
+            )
+            for i in range(X_TILES):
+                nc.scalar.copy(out=words[:, i, :, :, :], in_=flip(x_raw[:, i, :]))
+                nc.vector.quantize_mx(
+                    out=x_codes[:, i, :].bitcast(FP8X4),
+                    scales=x_scales[:, i, :],
+                    in_=x_grouped[:, i, :],
+                )
 
         def multiply_round(r):
             codes, scales = code_tiles[r]
@@ -141,19 +158,28 @@ def tile_grconv_pa_kernel(tc, x, x_mix, WL, WR, GL, GR, out):
                             stop=(side == SIDES - 1 and g == PASSES - 1),
                         )
 
+        def difference(chunk):
+            cols = slice(chunk * COLS, (chunk + 1) * COLS)
+            nc.vector.tensor_tensor(
+                out=blend[:, :, cols],
+                in0=mix_in[:, 1:X_TILES, cols],
+                in1=mix_in[:, 0:OUT_TILES, cols],
+                op=ALU.subtract,
+            )
+
         def epilogue(r, lag):
             kind, chunk = rounds[r]
             cols = slice(chunk * COLS, (chunk + 1) * COLS)
-            halves = [slice(2 * pair, 2 * pair + 2) for pair in range(PAIRS)]
+            both = [slice(2 * pair, 2 * pair + 2) for pair in range(PAIRS)]
             if kind == GATE0 and lag == 0:
                 for pair in range(PAIRS):
-                    nc.scalar.copy(out=ref[:, halves[pair], cols], in_=sum_tiles[r][pair][:])
+                    nc.scalar.copy(out=ref[:, both[pair], cols], in_=sum_tiles[r][pair][:])
             if kind == GATE1 and lag == 0:
                 for pair in range(PAIRS):
                     nc.vector.tensor_tensor(
-                        out=gap[:, halves[pair], cols],
+                        out=gap[:, both[pair], cols],
                         in0=sum_tiles[r][pair][:],
-                        in1=ref[:, halves[pair], cols],
+                        in1=ref[:, both[pair], cols],
                         op=ALU.subtract,
                     )
             if kind == GATE1 and lag == 1:
@@ -174,7 +200,11 @@ def tile_grconv_pa_kernel(tc, x, x_mix, WL, WR, GL, GR, out):
                     out=blend[:, :, cols], in0=share[:, :, cols], in1=blend[:, :, cols], op=ALU.mult
                 )
                 if r == last_gate1:
-                    nc.scalar.activation(out=gap[:], in_=gap[:], func=ACT.Ln, bias=plus_half[:])
+                    for c in range(CHUNKS):
+                        part = slice(c * COLS, (c + 1) * COLS)
+                        nc.scalar.activation(
+                            out=gap[:, :, part], in_=gap[:, :, part], func=ACT.Ln, bias=plus_half[:]
+                        )
             if kind == GATE1 and lag == 3:
                 nc.vector.tensor_tensor(
                     out=blend[:, :, cols],
@@ -185,9 +215,9 @@ def tile_grconv_pa_kernel(tc, x, x_mix, WL, WR, GL, GR, out):
             if kind == GATE2 and lag == 0:
                 for pair in range(PAIRS):
                     nc.vector.tensor_tensor(
-                        out=ref[:, halves[pair], cols],
+                        out=ref[:, both[pair], cols],
                         in0=sum_tiles[r][pair][:],
-                        in1=ref[:, halves[pair], cols],
+                        in1=ref[:, both[pair], cols],
                         op=ALU.subtract,
                     )
             if kind == GATE2 and lag == 2:
@@ -201,9 +231,9 @@ def tile_grconv_pa_kernel(tc, x, x_mix, WL, WR, GL, GR, out):
                 center_tiles[r] = center
                 for pair in range(PAIRS):
                     nc.scalar.activation(
-                        out=center[:, halves[pair], :], in_=sum_tiles[r][pair][:], func=ACT.Sigmoid
+                        out=center[:, both[pair], :], in_=sum_tiles[r][pair][:], func=ACT.Sigmoid
                     )
-            if kind == CENTER and lag == 1:
+            if kind == CENTER and lag == 2:
                 center = center_tiles[r]
                 nc.vector.tensor_tensor(
                     out=center[:], in0=center[:], in1=blend[:, :, cols], op=ALU.subtract
@@ -213,44 +243,36 @@ def tile_grconv_pa_kernel(tc, x, x_mix, WL, WR, GL, GR, out):
                 for op, other in ((ALU.mult, ref), (ALU.add, blend)):
                     for pair in range(PAIRS):
                         nc.vector.tensor_tensor(
-                            out=center[:, halves[pair], :],
-                            in0=center[:, halves[pair], :],
-                            in1=other[:, halves[pair], cols],
+                            out=center[:, both[pair], :],
+                            in0=center[:, both[pair], :],
+                            in1=other[:, both[pair], cols],
                             op=op,
                         )
                 nc.sync.dma_start(out=out_rows[:, :, cols], in_=center[:])
 
-        for i in range(X_TILES):
-            nc.sync.dma_start(out=x_raw[:, i, :], in_=x_rows[:, i, :])
         for r in range(RAW_BUFS):
             load_round(r)
-            if r == 1:
+            if r == 0:
+                for i in range(X_TILES):
+                    nc.sync.dma_start(out=x_raw[:, i, :], in_=x_rows[:, i, :])
+            if r == 3:
                 nc.sync.dma_start(out=mix_in[:], in_=mix_rows)
 
-        x_words = x_grouped[:].bitcast(F32).rearrange("p i (g r u) -> p i g r u", g=PASSES, u=HALVES)
-        for i in range(X_TILES):
-            nc.vector.tensor_copy(out=x_words[:, i, :, :, :], in_=flip(x_raw[:, i, :]))
-        for i in range(X_TILES):
-            nc.vector.quantize_mx(
-                out=x_codes[:, i, :].bitcast(FP8X4), scales=x_scales[:, i, :], in_=x_grouped[:, i, :]
-            )
-
-        max_lag = 3
-        for it in range(n_rounds + AHEAD + max_lag + 1):
+        for it in range(n_rounds + 2 + LAST_LAG + 1):
             if it < n_rounds:
                 transpose_round(it)
                 if it + RAW_BUFS < n_rounds:
                     load_round(it + RAW_BUFS)
+            if 0 <= it - 2 < n_rounds:
+                epilogue(it - 2, 0)
+            if 0 <= it - 3 < CHUNKS:
+                difference(it - 3)
+            for lag in range(1, LAST_LAG + 1):
+                if 0 <= it - 2 - lag < n_rounds:
+                    epilogue(it - 2 - lag, lag)
             if 0 <= it - 1 < n_rounds:
-                quantise_round(it - 1)
-            if 0 <= it - 1 < OUT_TILES:
-                i = it - 1
-                nc.vector.tensor_tensor(
-                    out=blend[:, i, :], in0=mix_in[:, i + 1, :], in1=mix_in[:, i, :], op=ALU.subtract
-                )
-            for lag in range(1, max_lag + 1):
-                if 0 <= it - AHEAD - lag < n_rounds:
-                    epilogue(it - AHEAD - lag, lag)
-            if 0 <= it - AHEAD < n_rounds:
-                multiply_round(it - AHEAD)
-                epilogue(it - AHEAD, 0)
+                multiply_round(it - 1)
+            if it < n_rounds:
+                quantise_round(it)
+            if it == 0:
+                prepare_x()

@@ -22,12 +22,15 @@ SIDES = 2
 COLS = 256
 ROW_TILES = COLS // P
 CHUNKS = H // COLS
-PAIRS = OUT_TILES // 2
+PER_BANK = 2
+BANKS = OUT_TILES // PER_BANK
 
 GATE0, GATE1, GATE2, CENTER = 0, 1, 2, 3
 
 RAW_BUFS = 6
+FIRST_STEP = 2
 LAST_LAG = 3
+MIX_AFTER = 3
 
 FLOPS = 2 * OUT_TILES * P * 4 * H * SIDES * K
 
@@ -44,7 +47,7 @@ def tile_grconv_pa_kernel(tc, x, x_mix, WL, WR, GL, GR, out):
         rounds.append((CENTER, chunk))
     n_rounds = len(rounds)
     last_gate1 = 2 * CHUNKS - 1
-    log_iteration = last_gate1 + 2 + 2
+    log_iteration = last_gate1 + FIRST_STEP + 2
 
     x_rows = x.rearrange("s a b k -> (a b) s k")
     mix_rows = x_mix.rearrange("s a b h -> (a b) s h")
@@ -56,7 +59,7 @@ def tile_grconv_pa_kernel(tc, x, x_mix, WL, WR, GL, GR, out):
         raw_pool = ctx.enter_context(tc.tile_pool(name="raw", bufs=RAW_BUFS))
         stage = ctx.enter_context(tc.tile_pool(name="stage", bufs=3))
         flip_banks = ctx.enter_context(tc.psum_pool(name="flip", bufs=4))
-        sum_banks = ctx.enter_context(tc.psum_pool(name="sums", bufs=4))
+        sum_banks = ctx.enter_context(tc.psum_pool(name="sums", bufs=2 * BANKS))
 
         identity = keep.tile([P, P], F32)
         make_identity(nc, identity[:])
@@ -88,11 +91,11 @@ def tile_grconv_pa_kernel(tc, x, x_mix, WL, WR, GL, GR, out):
             raw = raw_pool.tile([P, SIDES, ROW_TILES, K], BF16, name="raw")
             raw_tiles[r] = raw
             matrices = (WL, WR) if kind == CENTER else (GL, GR)
-            first = chunk * COLS if kind == CENTER else kind * H + chunk * COLS
+            top = chunk * COLS if kind == CENTER else kind * H + chunk * COLS
             for side in range(SIDES):
                 nc.sync.dma_start(
                     out=raw[:, side, :, :],
-                    in_=matrices[side][first : first + COLS, :].rearrange("(t p) k -> p t k", p=P),
+                    in_=matrices[side][top : top + COLS, :].rearrange("(t p) k -> p t k", p=P),
                 )
 
         def flip(rows):
@@ -100,8 +103,10 @@ def tile_grconv_pa_kernel(tc, x, x_mix, WL, WR, GL, GR, out):
             bank = flip_banks.tile([P, PASSES, HALVES, P], F32, name="bank")
             for g in range(PASSES):
                 for u in range(HALVES):
-                    first = (g * HALVES + u) * P
-                    nc.tensor.transpose(bank[:, g, u, :], words[:, first : first + P], identity[:])
+                    left_word = (g * HALVES + u) * P
+                    nc.tensor.transpose(
+                        bank[:, g, u, :], words[:, left_word : left_word + P], identity[:]
+                    )
             return bank[:].rearrange("p g u r -> p g r u")
 
         def transpose_round(r):
@@ -141,7 +146,7 @@ def tile_grconv_pa_kernel(tc, x, x_mix, WL, WR, GL, GR, out):
 
         def multiply_round(r):
             codes, scales = code_tiles[r]
-            sums = [sum_banks.tile([P, 2, COLS], F32, name="sums") for pair in range(PAIRS)]
+            sums = [sum_banks.tile([P, PER_BANK, COLS], F32, name="sums") for bank in range(BANKS)]
             sum_tiles[r] = sums
             for i in range(OUT_TILES):
                 for side in range(SIDES):
@@ -149,7 +154,7 @@ def tile_grconv_pa_kernel(tc, x, x_mix, WL, WR, GL, GR, out):
                         tokens = slice(g * P, (g + 1) * P)
                         feats = slice((side * PASSES + g) * COLS, (side * PASSES + g + 1) * COLS)
                         nc.tensor.matmul_mx(
-                            out=sums[i // 2][:, i % 2, :],
+                            out=sums[i // PER_BANK][:, i % PER_BANK, :],
                             lhsT=x_codes[:, i + side, tokens].bitcast(FP8X4),
                             lhsT_scale=x_scales[:, i + side, tokens],
                             rhs=codes[:, feats].bitcast(FP8X4),
@@ -167,19 +172,19 @@ def tile_grconv_pa_kernel(tc, x, x_mix, WL, WR, GL, GR, out):
                 op=ALU.subtract,
             )
 
-        def epilogue(r, lag):
+        def elementwise(r, lag):
             kind, chunk = rounds[r]
             cols = slice(chunk * COLS, (chunk + 1) * COLS)
-            both = [slice(2 * pair, 2 * pair + 2) for pair in range(PAIRS)]
+            held = [slice(PER_BANK * bank, PER_BANK * (bank + 1)) for bank in range(BANKS)]
             if kind == GATE0 and lag == 0:
-                for pair in range(PAIRS):
-                    nc.scalar.copy(out=ref[:, both[pair], cols], in_=sum_tiles[r][pair][:])
+                for bank in range(BANKS):
+                    nc.scalar.copy(out=ref[:, held[bank], cols], in_=sum_tiles[r][bank][:])
             if kind == GATE1 and lag == 0:
-                for pair in range(PAIRS):
+                for bank in range(BANKS):
                     nc.vector.tensor_tensor(
-                        out=gap[:, both[pair], cols],
-                        in0=sum_tiles[r][pair][:],
-                        in1=ref[:, both[pair], cols],
+                        out=gap[:, held[bank], cols],
+                        in0=sum_tiles[r][bank][:],
+                        in1=ref[:, held[bank], cols],
                         op=ALU.subtract,
                     )
             if kind == GATE1 and lag == 1:
@@ -200,8 +205,8 @@ def tile_grconv_pa_kernel(tc, x, x_mix, WL, WR, GL, GR, out):
                     out=blend[:, :, cols], in0=share[:, :, cols], in1=blend[:, :, cols], op=ALU.mult
                 )
                 if r == last_gate1:
-                    for c in range(CHUNKS):
-                        part = slice(c * COLS, (c + 1) * COLS)
+                    for every in range(CHUNKS):
+                        part = slice(every * COLS, (every + 1) * COLS)
                         nc.scalar.activation(
                             out=gap[:, :, part], in_=gap[:, :, part], func=ACT.Ln, bias=plus_half[:]
                         )
@@ -213,11 +218,11 @@ def tile_grconv_pa_kernel(tc, x, x_mix, WL, WR, GL, GR, out):
                     op=ALU.add,
                 )
             if kind == GATE2 and lag == 0:
-                for pair in range(PAIRS):
+                for bank in range(BANKS):
                     nc.vector.tensor_tensor(
-                        out=ref[:, both[pair], cols],
-                        in0=sum_tiles[r][pair][:],
-                        in1=ref[:, both[pair], cols],
+                        out=ref[:, held[bank], cols],
+                        in0=sum_tiles[r][bank][:],
+                        in1=ref[:, held[bank], cols],
                         op=ALU.subtract,
                     )
             if kind == GATE2 and lag == 2:
@@ -229,9 +234,9 @@ def tile_grconv_pa_kernel(tc, x, x_mix, WL, WR, GL, GR, out):
             if kind == CENTER and lag == 0:
                 center = stage.tile([P, OUT_TILES, COLS], F32, name="center")
                 center_tiles[r] = center
-                for pair in range(PAIRS):
+                for bank in range(BANKS):
                     nc.scalar.activation(
-                        out=center[:, both[pair], :], in_=sum_tiles[r][pair][:], func=ACT.Sigmoid
+                        out=center[:, held[bank], :], in_=sum_tiles[r][bank][:], func=ACT.Sigmoid
                     )
             if kind == CENTER and lag == 2:
                 center = center_tiles[r]
@@ -240,36 +245,42 @@ def tile_grconv_pa_kernel(tc, x, x_mix, WL, WR, GL, GR, out):
                 )
             if kind == CENTER and lag == 3:
                 center = center_tiles[r]
-                for op, other in ((ALU.mult, ref), (ALU.add, blend)):
-                    for pair in range(PAIRS):
-                        nc.vector.tensor_tensor(
-                            out=center[:, both[pair], :],
-                            in0=center[:, both[pair], :],
-                            in1=other[:, both[pair], cols],
-                            op=op,
-                        )
-                nc.sync.dma_start(out=out_rows[:, :, cols], in_=center[:])
+                for bank in range(BANKS):
+                    nc.vector.tensor_tensor(
+                        out=center[:, held[bank], :],
+                        in0=center[:, held[bank], :],
+                        in1=ref[:, held[bank], cols],
+                        op=ALU.mult,
+                    )
+                for bank in range(BANKS):
+                    nc.vector.tensor_tensor(
+                        out=center[:, held[bank], :],
+                        in0=center[:, held[bank], :],
+                        in1=blend[:, held[bank], cols],
+                        op=ALU.add,
+                    )
+                    nc.sync.dma_start(out=out_rows[:, held[bank], cols], in_=center[:, held[bank], :])
 
         for r in range(RAW_BUFS):
             load_round(r)
             if r == 0:
                 for i in range(X_TILES):
                     nc.sync.dma_start(out=x_raw[:, i, :], in_=x_rows[:, i, :])
-            if r == 3:
+            if r == MIX_AFTER:
                 nc.sync.dma_start(out=mix_in[:], in_=mix_rows)
 
-        for it in range(n_rounds + 2 + LAST_LAG + 1):
+        for it in range(n_rounds + FIRST_STEP + LAST_LAG + 1):
             if it < n_rounds:
                 transpose_round(it)
                 if it + RAW_BUFS < n_rounds:
                     load_round(it + RAW_BUFS)
-            if 0 <= it - 2 < n_rounds:
-                epilogue(it - 2, 0)
-            if 0 <= it - 3 < CHUNKS:
-                difference(it - 3)
+            if 0 <= it - FIRST_STEP < n_rounds:
+                elementwise(it - FIRST_STEP, 0)
+            if 0 <= it - MIX_AFTER < CHUNKS:
+                difference(it - MIX_AFTER)
             for lag in range(1, LAST_LAG + 1):
-                if 0 <= it - 2 - lag < n_rounds:
-                    epilogue(it - 2 - lag, lag)
+                if 0 <= it - FIRST_STEP - lag < n_rounds:
+                    elementwise(it - FIRST_STEP - lag, lag)
             if 0 <= it - 1 < n_rounds:
                 multiply_round(it - 1)
             if it < n_rounds:

from contextlib import ExitStack

import concourse.mybir as mybir
from concourse.masks import make_identity

F32 = mybir.dt.float32
BF16 = mybir.dt.bfloat16
U32 = mybir.dt.uint32
U8 = mybir.dt.uint8
FP8X4 = mybir.dt.float8_e4m3fn_x4
ACT = mybir.ActivationFunctionType
ALU = mybir.AluOpType

P = 128
K = 1024
H = 1024
PASSES = 2
HALVES = 2
OUT_TILES = 4
X_TILES = 5
SIDES = 2
COLS = 256
ROW_TILES = COLS // P
CHUNKS = H // COLS
PER_BANK = 2
BANKS = OUT_TILES // PER_BANK

GATE0, GATE1, GATE2, CENTER = 0, 1, 2, 3

RAW_BUFS = 6
FIRST_STEP = 2
LAST_LAG = 3
MIX_AFTER = 3

FLOPS = 2 * OUT_TILES * P * 4 * H * SIDES * K


def tile_grconv_pa_kernel(tc, x, x_mix, WL, WR, GL, GR, out):
    nc = tc.nc

    rounds = []
    for chunk in range(CHUNKS):
        rounds.append((GATE0, chunk))
        rounds.append((GATE1, chunk))
    for chunk in range(CHUNKS):
        rounds.append((GATE2, chunk))
        rounds.append((CENTER, chunk))
    n_rounds = len(rounds)
    last_gate1 = 2 * CHUNKS - 1
    log_iteration = last_gate1 + FIRST_STEP + 2

    x_rows = x.rearrange("s a b k -> (a b) s k")
    mix_rows = x_mix.rearrange("s a b h -> (a b) s h")
    out_rows = out.rearrange("s a b h -> (a b) s h")

    with ExitStack() as ctx:
        ctx.enter_context(tc.manual_schedule())
        keep = ctx.enter_context(tc.tile_pool(name="keep", bufs=1))
        raw_pool = ctx.enter_context(tc.tile_pool(name="raw", bufs=RAW_BUFS))
        stage = ctx.enter_context(tc.tile_pool(name="stage", bufs=3))
        flip_banks = ctx.enter_context(tc.psum_pool(name="flip", bufs=4))
        sum_banks = ctx.enter_context(tc.psum_pool(name="sums", bufs=2 * BANKS))

        identity = keep.tile([P, P], F32)
        make_identity(nc, identity[:])
        minus_half = keep.tile([P, 1], F32)
        nc.vector.memset(minus_half[:], -0.5)
        plus_half = keep.tile([P, 1], F32)
        nc.vector.memset(plus_half[:], 0.5)
        warm = keep.tile([P, 1], F32)
        nc.scalar.activation(out=warm[:], in_=plus_half[:], func=ACT.Sigmoid)

        x_raw = keep.tile([P, X_TILES, K], BF16)
        x_grouped = keep.tile([P, X_TILES, K], BF16, align_bytes=64)
        x_codes = keep.tile([P, X_TILES, K // 4], U32, align_bytes=64)
        x_scales = keep.tile([P, X_TILES, K // 4], U8, align_bytes=64)
        mix_in = keep.tile([P, X_TILES, H], BF16)
        ref = keep.tile([P, OUT_TILES, H], F32)
        gap = keep.tile([P, OUT_TILES, H], F32)
        share = keep.tile([P, OUT_TILES, H], F32)
        blend = keep.tile([P, OUT_TILES, H], F32)

        raw_tiles = {}
        grouped_tiles = {}
        code_tiles = {}
        sum_tiles = {}
        center_tiles = {}

        def load_round(r):
            kind, chunk = rounds[r]
            raw = raw_pool.tile([P, SIDES, ROW_TILES, K], BF16, name="raw")
            raw_tiles[r] = raw
            matrices = (WL, WR) if kind == CENTER else (GL, GR)
            top = chunk * COLS if kind == CENTER else kind * H + chunk * COLS
            for side in range(SIDES):
                nc.sync.dma_start(
                    out=raw[:, side, :, :],
                    in_=matrices[side][top : top + COLS, :].rearrange("(t p) k -> p t k", p=P),
                )

        def flip(rows):
            words = rows.bitcast(F32)
            bank = flip_banks.tile([P, PASSES, HALVES, P], F32, name="bank")
            for g in range(PASSES):
                for u in range(HALVES):
                    left_word = (g * HALVES + u) * P
                    nc.tensor.transpose(
                        bank[:, g, u, :], words[:, left_word : left_word + P], identity[:]
                    )
            return bank[:].rearrange("p g u r -> p g r u")

        def transpose_round(r):
            grouped = stage.tile([P, SIDES * PASSES * COLS * 4], BF16, align_bytes=64, name="grouped")
            grouped_tiles[r] = grouped
            words = grouped[:].bitcast(F32).rearrange(
                "p (s g f u) -> p s g f u", s=SIDES, g=PASSES, u=HALVES
            )
            for side in range(SIDES):
                for t in range(ROW_TILES):
                    flipped = flip(raw_tiles[r][:, side, t, :])
                    target = words[:, side, :, t * P : (t + 1) * P, :]
                    if r == log_iteration:
                        nc.vector.tensor_copy(out=target, in_=flipped)
                    else:
                        nc.scalar.copy(out=target, in_=flipped)

        def quantise_round(r):
            codes = stage.tile([P, SIDES * PASSES * COLS], U32, align_bytes=64, name="codes")
            scales = stage.tile([P, SIDES * PASSES * COLS], U8, align_bytes=64, name="scales")
            code_tiles[r] = (codes, scales)
            nc.vector.quantize_mx(
                out=codes[:].bitcast(FP8X4), scales=scales[:], in_=grouped_tiles[r][:]
            )

        def prepare_x():
            words = x_grouped[:].bitcast(F32).rearrange(
                "p i (g r u) -> p i g r u", g=PASSES, u=HALVES
            )
            for i in range(X_TILES):
                nc.scalar.copy(out=words[:, i, :, :, :], in_=flip(x_raw[:, i, :]))
                nc.vector.quantize_mx(
                    out=x_codes[:, i, :].bitcast(FP8X4),
                    scales=x_scales[:, i, :],
                    in_=x_grouped[:, i, :],
                )

        def multiply_round(r):
            codes, scales = code_tiles[r]
            sums = [sum_banks.tile([P, PER_BANK, COLS], F32, name="sums") for bank in range(BANKS)]
            sum_tiles[r] = sums
            for i in range(OUT_TILES):
                for side in range(SIDES):
                    for g in range(PASSES):
                        tokens = slice(g * P, (g + 1) * P)
                        feats = slice((side * PASSES + g) * COLS, (side * PASSES + g + 1) * COLS)
                        nc.tensor.matmul_mx(
                            out=sums[i // PER_BANK][:, i % PER_BANK, :],
                            lhsT=x_codes[:, i + side, tokens].bitcast(FP8X4),
                            lhsT_scale=x_scales[:, i + side, tokens],
                            rhs=codes[:, feats].bitcast(FP8X4),
                            rhs_scale=scales[:, feats],
                            start=(side == 0 and g == 0),
                            stop=(side == SIDES - 1 and g == PASSES - 1),
                        )

        def difference(chunk):
            cols = slice(chunk * COLS, (chunk + 1) * COLS)
            nc.vector.tensor_tensor(
                out=blend[:, :, cols],
                in0=mix_in[:, 1:X_TILES, cols],
                in1=mix_in[:, 0:OUT_TILES, cols],
                op=ALU.subtract,
            )

        def elementwise(r, lag):
            kind, chunk = rounds[r]
            cols = slice(chunk * COLS, (chunk + 1) * COLS)
            held = [slice(PER_BANK * bank, PER_BANK * (bank + 1)) for bank in range(BANKS)]
            if kind == GATE0 and lag == 0:
                for bank in range(BANKS):
                    nc.scalar.copy(out=ref[:, held[bank], cols], in_=sum_tiles[r][bank][:])
            if kind == GATE1 and lag == 0:
                for bank in range(BANKS):
                    nc.vector.tensor_tensor(
                        out=gap[:, held[bank], cols],
                        in0=sum_tiles[r][bank][:],
                        in1=ref[:, held[bank], cols],
                        op=ALU.subtract,
                    )
            if kind == GATE1 and lag == 1:
                nc.vector.scalar_tensor_tensor(
                    out=ref[:, :, cols],
                    in0=gap[:, :, cols],
                    scalar=0.0,
                    in1=ref[:, :, cols],
                    op0=ALU.max,
                    op1=ALU.add,
                )
                nc.scalar.activation(out=share[:, :, cols], in_=gap[:, :, cols], func=ACT.Sigmoid)
            if kind == GATE1 and lag == 2:
                nc.scalar.activation(
                    out=gap[:, :, cols], in_=share[:, :, cols], func=ACT.Abs, bias=minus_half[:]
                )
                nc.vector.tensor_tensor(
                    out=blend[:, :, cols], in0=share[:, :, cols], in1=blend[:, :, cols], op=ALU.mult
                )
                if r == last_gate1:
                    for every in range(CHUNKS):
                        part = slice(every * COLS, (every + 1) * COLS)
                        nc.scalar.activation(
                            out=gap[:, :, part], in_=gap[:, :, part], func=ACT.Ln, bias=plus_half[:]
                        )
            if kind == GATE1 and lag == 3:
                nc.vector.tensor_tensor(
                    out=blend[:, :, cols],
                    in0=blend[:, :, cols],
                    in1=mix_in[:, 0:OUT_TILES, cols],
                    op=ALU.add,
                )
            if kind == GATE2 and lag == 0:
                for bank in range(BANKS):
                    nc.vector.tensor_tensor(
                        out=ref[:, held[bank], cols],
                        in0=sum_tiles[r][bank][:],
                        in1=ref[:, held[bank], cols],
                        op=ALU.subtract,
                    )
            if kind == GATE2 and lag == 2:
                nc.vector.tensor_tensor(
                    out=ref[:, :, cols], in0=ref[:, :, cols], in1=gap[:, :, cols], op=ALU.add
                )
            if kind == GATE2 and lag == 3:
                nc.scalar.activation(out=ref[:, :, cols], in_=ref[:, :, cols], func=ACT.Sigmoid)
            if kind == CENTER and lag == 0:
                center = stage.tile([P, OUT_TILES, COLS], F32, name="center")
                center_tiles[r] = center
                for bank in range(BANKS):
                    nc.scalar.activation(
                        out=center[:, held[bank], :], in_=sum_tiles[r][bank][:], func=ACT.Sigmoid
                    )
            if kind == CENTER and lag == 2:
                center = center_tiles[r]
                nc.vector.tensor_tensor(
                    out=center[:], in0=center[:], in1=blend[:, :, cols], op=ALU.subtract
                )
            if kind == CENTER and lag == 3:
                center = center_tiles[r]
                for bank in range(BANKS):
                    nc.vector.tensor_tensor(
                        out=center[:, held[bank], :],
                        in0=center[:, held[bank], :],
                        in1=ref[:, held[bank], cols],
                        op=ALU.mult,
                    )
                for bank in range(BANKS):
                    nc.vector.tensor_tensor(
                        out=center[:, held[bank], :],
                        in0=center[:, held[bank], :],
                        in1=blend[:, held[bank], cols],
                        op=ALU.add,
                    )
                    nc.sync.dma_start(out=out_rows[:, held[bank], cols], in_=center[:, held[bank], :])

        for r in range(RAW_BUFS):
            load_round(r)
            if r == 0:
                for i in range(X_TILES):
                    nc.sync.dma_start(out=x_raw[:, i, :], in_=x_rows[:, i, :])
            if r == MIX_AFTER:
                nc.sync.dma_start(out=mix_in[:], in_=mix_rows)

        for it in range(n_rounds + FIRST_STEP + LAST_LAG + 1):
            if it < n_rounds:
                transpose_round(it)
                if it + RAW_BUFS < n_rounds:
                    load_round(it + RAW_BUFS)
            if 0 <= it - FIRST_STEP < n_rounds:
                elementwise(it - FIRST_STEP, 0)
            if 0 <= it - MIX_AFTER < CHUNKS:
                difference(it - MIX_AFTER)
            for lag in range(1, LAST_LAG + 1):
                if 0 <= it - FIRST_STEP - lag < n_rounds:
                    elementwise(it - FIRST_STEP - lag, lag)
            if 0 <= it - 1 < n_rounds:
                multiply_round(it - 1)
            if it < n_rounds:
                quantise_round(it)
            if it == 0:
                prepare_x()
